import numpy as np
import ml_dtypes


def mxq(x, axis, fmt="e4m3"):
    dtype, down = {"e4m3": (ml_dtypes.float8_e4m3fn, 7), "e5m2": (ml_dtypes.float8_e5m2, 14)}[fmt]
    v = np.moveaxis(np.asarray(x, np.float32).astype(ml_dtypes.bfloat16).astype(np.float64), axis, -1)
    blocks = v.reshape(v.shape[:-1] + (-1, 32))
    amax = np.abs(blocks).max(-1, keepdims=True)
    byte = np.maximum(np.where(amax > 0, np.frexp(amax)[1] - 1 + 127, 0) - down, 1)
    scale = np.exp2(byte - 127.0)
    codes = (blocks / scale).astype(np.float32).astype(dtype).astype(np.float64)
    return np.moveaxis((codes * scale).reshape(v.shape), -1, axis)


WIDE = False


def mx_kscale(k):
    if not WIDE:
        return np.ones(k)
    levels = np.array([20, -20, 10, -10, 0])
    a = np.random.permutation(np.resize(levels, k // 512 * 4)).reshape(k // 512, 4)
    idx = np.arange(k)
    return np.exp2(a[idx // 512, idx % 128 // 32])


BF16 = ml_dtypes.bfloat16


def bf(x):
    return np.asarray(x, np.float32).astype(BF16)


def f64(x):
    return np.asarray(x).astype(np.float64)


B, NH, T, D, N = 1, 1, 256, 512, 8192
THETA = 2.0 ** 16
SCALE = N ** -0.5


def rope_tables():
    pair = np.repeat(np.arange(N // 2), 2)
    freqs = 1.0 / THETA ** (pair * 2.0 / N)
    angles = np.arange(T)[:, None] * freqs[None, :]
    return np.cos(angles), np.sin(angles)


def rope(v, cos, sin):
    v_rot = np.stack([-v[..., 1::2], v[..., ::2]], axis=-1).reshape(v.shape)
    return v * cos + v_rot * sin


def setup_inputs():
    s = np.repeat(mx_kscale(N)[::2], 2)
    cos, sin = rope_tables()
    Q = np.random.uniform(size=(B, NH, T, N)) * 1.2 / N ** 0.25 * s[None, :]
    V = np.random.standard_normal((B, 1, T, D)) * 45.0 / np.sqrt(T)
    state = np.random.standard_normal((B, NH, N, D)) * 60.0 / N ** 0.75
    g = np.random.standard_normal((B, NH, N, D)) * np.exp2(np.random.randint(-12, 1, (B, NH, N, 1))) * 64.0 / s[:, None]
    return {"Q": bf(Q), "V": bf(V), "state": bf(state),
            "cos": bf(cos), "sin": bf(sin), "grad_out": bf(g)}


def reference(Q, V, state, cos, sin, grad_out):
    QR = rope(f64(Q), f64(cos), f64(sin))
    gv = (mxq(QR, 3, "e4m3") @ mxq(f64(grad_out), 2, "e5m2")) * SCALE
    return gv.sum(axis=1, keepdims=True)

@@ -1,0 +1,174 @@
+from contextlib import ExitStack
+
+import concourse.mybir as mybir
+from concourse.masks import make_identity
+
+BF16 = mybir.dt.bfloat16
+F32 = mybir.dt.float32
+U32 = mybir.dt.uint32
+U8 = mybir.dt.uint8
+E4M3_X4 = mybir.dt.float8_e4m3fn_x4
+E5M2_X4 = mybir.dt.float8_e5m2_x4
+MULT = mybir.AluOpType.mult
+
+P = 128
+PACK = 4
+K_PASS = P * PACK
+TOKENS = 256
+FEATURES = 8192
+VALUES = 512
+TOKEN_TILES = TOKENS // P
+PASSES = FEATURES // K_PASS
+SCALE = FEATURES**-0.5
+
+LOAD_FEATURES = 2048
+ROUND_PASSES = 2
+ROUND_FEATURES = ROUND_PASSES * K_PASS
+ROUNDS = PASSES // ROUND_PASSES
+ROUNDS_PER_LOAD = LOAD_FEATURES // ROUND_FEATURES
+HALVES = 2 * ROUND_PASSES
+
+FLOPS = 2 * TOKENS * FEATURES * VALUES
+BYTES = 2 * (3 * TOKENS * FEATURES + FEATURES * VALUES) + 4 * TOKENS * VALUES
+
+
+def tile_attention_pb_kernel(tc, Q, V, state, cos, sin, grad_out, out):
+    nc = tc.nc
+    q_dram = Q.flatten_outer_dims()
+    g_dram = grad_out.flatten_outer_dims()
+    out_dram = out.flatten_outer_dims()
+
+    with ExitStack() as pools:
+        const = pools.enter_context(tc.tile_pool(name="const", bufs=1))
+        rope_in = pools.enter_context(tc.tile_pool(name="rope_in", bufs=4))
+        grad_in = pools.enter_context(tc.tile_pool(name="grad_in", bufs=8))
+        planes = pools.enter_context(tc.tile_pool(name="planes", bufs=3))
+        grouped = pools.enter_context(tc.tile_pool(name="grouped", bufs=4))
+        packed = pools.enter_context(tc.tile_pool(name="packed", bufs=4))
+        result = pools.enter_context(tc.tile_pool(name="result", bufs=1))
+        flipped = pools.enter_context(tc.psum_pool(name="flipped", bufs=6))
+        sums = pools.enter_context(tc.psum_pool(name="sums", bufs=1))
+
+        identity = const.tile([P, P], F32)
+        make_identity(nc, identity[:])
+
+        acc = []
+        for tt in range(TOKEN_TILES):
+            acc_tile = sums.tile([P, VALUES], F32, name="acc%d" % tt)
+            acc.append(acc_tile)
+
+        rope_tiles = {}
+        for r in range(ROUNDS):
+            grad_tiles = []
+            for i in range(ROUND_PASSES):
+                if r % ROUNDS_PER_LOAD == 0 and i < TOKEN_TILES:
+                    tt = i
+                    rows = slice(tt * P, (tt + 1) * P)
+                    cols = slice(r * ROUND_FEATURES, r * ROUND_FEATURES + LOAD_FEATURES)
+                    q_in = rope_in.tile([P, LOAD_FEATURES], BF16)
+                    nc.sync.dma_start(out=q_in[:], in_=q_dram[rows, cols])
+                    cos_in = rope_in.tile([P, LOAD_FEATURES], BF16)
+                    nc.sync.dma_start(out=cos_in[:], in_=cos[rows, cols])
+                    sin_in = rope_in.tile([P, LOAD_FEATURES], BF16)
+                    nc.sync.dma_start(out=sin_in[:], in_=sin[rows, cols])
+                    rope_tiles[tt] = (q_in, cos_in, sin_in)
+                g = r * ROUND_PASSES + i
+                g_in = grad_in.tile([P, PACK, VALUES], BF16)
+                nc.sync.dma_start(
+                    out=g_in[:].rearrange("p (u e) d -> p u e d", u=2),
+                    in_=g_dram[g * K_PASS : (g + 1) * K_PASS, :].rearrange(
+                        "(u p e) d -> p u e d", u=2, p=P, e=2
+                    ),
+                )
+                grad_tiles.append(g_in)
+
+            first = (r % ROUNDS_PER_LOAD) * ROUND_FEATURES
+            qr_grouped = []
+            for i in range(ROUND_PASSES):
+                qr_bf = grouped.tile([P, TOKEN_TILES, P, PACK], BF16, align_bytes=64)
+                qr_grouped.append(qr_bf)
+            for tt in range(TOKEN_TILES):
+                q_v, cos_v, sin_v = [
+                    t[:, first : first + ROUND_FEATURES].rearrange(
+                        "t (h p e) -> t h e p", h=HALVES, p=P, e=2
+                    )
+                    for t in rope_tiles[tt]
+                ]
+                direct = planes.tile([P, HALVES, 2, P], F32)
+                nc.vector.tensor_tensor(out=direct[:], in0=q_v, in1=cos_v, op=MULT)
+                crossed = planes.tile([P, HALVES, 2, P], F32)
+                nc.vector.tensor_tensor(
+                    out=crossed[:, :, 1, :], in0=q_v[:, :, 0, :], in1=sin_v[:, :, 1, :], op=MULT
+                )
+                nc.vector.scalar_tensor_tensor(
+                    out=crossed[:, :, 0, :],
+                    in0=q_v[:, :, 1, :],
+                    scalar=-1.0,
+                    in1=sin_v[:, :, 0, :],
+                    op0=MULT,
+                    op1=MULT,
+                )
+                for i in range(ROUND_PASSES):
+                    qr_t = flipped.tile([P, PACK, P], F32)
+                    for u in range(2):
+                        for e in range(2):
+                            h = 2 * i + u
+                            nc.tensor.matmul(
+                                out=qr_t[:, 2 * u + e, :],
+                                lhsT=direct[:, h, e, :],
+                                rhs=identity[:],
+                                is_transpose=True,
+                                start=True,
+                                stop=False,
+                            )
+                            nc.tensor.matmul(
+                                out=qr_t[:, 2 * u + e, :],
+                                lhsT=crossed[:, h, e, :],
+                                rhs=identity[:],
+                                is_transpose=True,
+                                start=False,
+                                stop=True,
+                            )
+                    nc.scalar.copy(
+                        out=qr_grouped[i][:, tt, :, :], in_=qr_t[:].rearrange("p j t -> p t j")
+                    )
+
+            for i in range(ROUND_PASSES):
+                g = r * ROUND_PASSES + i
+                g_bf = grouped.tile([P, VALUES, PACK], BF16, align_bytes=64)
+                nc.scalar.copy(
+                    out=g_bf[:].rearrange("p (c i) j -> p c j i", i=4),
+                    in_=grad_tiles[i][:].rearrange("p j (c i) -> p c j i", i=4),
+                )
+                g_codes = packed.tile([P, VALUES], U32, align_bytes=64)
+                g_scales = packed.tile([P, VALUES], U8, align_bytes=64)
+                nc.vector.quantize_mx(
+                    out=g_codes[:].bitcast(E5M2_X4),
+                    scales=g_scales[:],
+                    in_=g_bf[:].rearrange("p d j -> p (d j)"),
+                )
+                q_codes = packed.tile([P, TOKENS], U32, align_bytes=64)
+                q_scales = packed.tile([P, TOKENS], U8, align_bytes=64)
+                nc.vector.quantize_mx(
+                    out=q_codes[:].bitcast(E4M3_X4),
+                    scales=q_scales[:],
+                    in_=qr_grouped[i][:].rearrange("p a t j -> p (a t j)"),
+                )
+                for tt in range(TOKEN_TILES):
+                    tok = slice(tt * P, (tt + 1) * P)
+                    nc.tensor.matmul_mx(
+                        out=acc[tt][:],
+                        lhsT=q_codes[:, tok].bitcast(E4M3_X4),
+                        lhsT_scale=q_scales[:, tok],
+                        rhs=g_codes[:].bitcast(E5M2_X4),
+                        rhs_scale=g_scales[:],
+                        start=(g == 0),
+                        stop=(g == PASSES - 1),
+                    )
+
+        out0 = result.tile([P, VALUES], F32)
+        nc.vector.tensor_scalar_mul(out=out0[:], in0=acc[0][:], scalar1=SCALE)
+        nc.sync.dma_start(out=out_dram[0:P, :], in_=out0[:])
+        out1 = result.tile([P, VALUES], F32)
+        nc.scalar.mul(out=out1[:], in_=acc[1][:], mul=SCALE)
+        nc.sync.dma_start(out=out_dram[P : 2 * P, :], in_=out1[:])

@@ -21,12 +21,13 @@ TOKEN_TILES = TOKENS // P
 PASSES = FEATURES // K_PASS
 SCALE = FEATURES**-0.5
 
-LOAD_FEATURES = 2048
-ROUND_PASSES = 2
-ROUND_FEATURES = ROUND_PASSES * K_PASS
-ROUNDS = PASSES // ROUND_PASSES
-ROUNDS_PER_LOAD = LOAD_FEATURES // ROUND_FEATURES
-HALVES = 2 * ROUND_PASSES
+STEP_PASSES = 2
+STEP_FEATURES = STEP_PASSES * K_PASS
+STEPS = TOKEN_TILES * PASSES // STEP_PASSES
+HALVES = 2 * STEP_PASSES
+LOAD_FEATURES = 2 * STEP_FEATURES
+LOAD_STEPS = TOKEN_TILES * LOAD_FEATURES // STEP_FEATURES
+LOAD_AHEAD = 4
 
 FLOPS = 2 * TOKENS * FEATURES * VALUES
 BYTES = 2 * (3 * TOKENS * FEATURES + FEATURES * VALUES) + 4 * TOKENS * VALUES
@@ -41,10 +42,11 @@ def tile_attention_pb_kernel(tc, Q, V, state, cos, sin, grad_out, out):
     with ExitStack() as pools:
         const = pools.enter_context(tc.tile_pool(name="const", bufs=1))
         rope_in = pools.enter_context(tc.tile_pool(name="rope_in", bufs=4))
-        grad_in = pools.enter_context(tc.tile_pool(name="grad_in", bufs=8))
+        grad_in = pools.enter_context(tc.tile_pool(name="grad_in", bufs=LOAD_AHEAD + 2))
         planes = pools.enter_context(tc.tile_pool(name="planes", bufs=3))
-        grouped = pools.enter_context(tc.tile_pool(name="grouped", bufs=4))
-        packed = pools.enter_context(tc.tile_pool(name="packed", bufs=4))
+        grouped = pools.enter_context(tc.tile_pool(name="grouped", bufs=3))
+        grad_mx = pools.enter_context(tc.tile_pool(name="grad_mx", bufs=6))
+        rope_mx = pools.enter_context(tc.tile_pool(name="rope_mx", bufs=3))
         result = pools.enter_context(tc.tile_pool(name="result", bufs=1))
         flipped = pools.enter_context(tc.psum_pool(name="flipped", bufs=6))
         sums = pools.enter_context(tc.psum_pool(name="sums", bufs=1))
@@ -57,118 +59,161 @@ def tile_attention_pb_kernel(tc, Q, V, state, cos, sin, grad_out, out):
             acc_tile = sums.tile([P, VALUES], F32, name="acc%d" % tt)
             acc.append(acc_tile)
 
-        rope_tiles = {}
-        for r in range(ROUNDS):
-            grad_tiles = []
-            for i in range(ROUND_PASSES):
-                if r % ROUNDS_PER_LOAD == 0 and i < TOKEN_TILES:
-                    tt = i
-                    rows = slice(tt * P, (tt + 1) * P)
-                    cols = slice(r * ROUND_FEATURES, r * ROUND_FEATURES + LOAD_FEATURES)
-                    q_in = rope_in.tile([P, LOAD_FEATURES], BF16)
-                    nc.sync.dma_start(out=q_in[:], in_=q_dram[rows, cols])
-                    cos_in = rope_in.tile([P, LOAD_FEATURES], BF16)
-                    nc.sync.dma_start(out=cos_in[:], in_=cos[rows, cols])
-                    sin_in = rope_in.tile([P, LOAD_FEATURES], BF16)
-                    nc.sync.dma_start(out=sin_in[:], in_=sin[rows, cols])
-                    rope_tiles[tt] = (q_in, cos_in, sin_in)
-                g = r * ROUND_PASSES + i
-                g_in = grad_in.tile([P, PACK, VALUES], BF16)
-                nc.sync.dma_start(
-                    out=g_in[:].rearrange("p (u e) d -> p u e d", u=2),
-                    in_=g_dram[g * K_PASS : (g + 1) * K_PASS, :].rearrange(
-                        "(u p e) d -> p u e d", u=2, p=P, e=2
-                    ),
-                )
-                grad_tiles.append(g_in)
+        rope_loaded = {}
+        grad_loaded = {}
+        products = {}
+        banks = {}
+        rope_bf = {}
+        grad_bf = {}
+        rope_packed = {}
+        grad_packed = {}
 
-            first = (r % ROUNDS_PER_LOAD) * ROUND_FEATURES
-            qr_grouped = []
-            for i in range(ROUND_PASSES):
-                qr_bf = grouped.tile([P, TOKEN_TILES, P, PACK], BF16, align_bytes=64)
-                qr_grouped.append(qr_bf)
-            for tt in range(TOKEN_TILES):
-                q_v, cos_v, sin_v = [
-                    t[:, first : first + ROUND_FEATURES].rearrange(
-                        "t (h p e) -> t h e p", h=HALVES, p=P, e=2
-                    )
-                    for t in rope_tiles[tt]
-                ]
-                direct = planes.tile([P, HALVES, 2, P], F32)
-                nc.vector.tensor_tensor(out=direct[:], in0=q_v, in1=cos_v, op=MULT)
-                crossed = planes.tile([P, HALVES, 2, P], F32)
-                nc.vector.tensor_tensor(
-                    out=crossed[:, :, 1, :], in0=q_v[:, :, 0, :], in1=sin_v[:, :, 1, :], op=MULT
-                )
-                nc.vector.scalar_tensor_tensor(
-                    out=crossed[:, :, 0, :],
-                    in0=q_v[:, :, 1, :],
-                    scalar=-1.0,
-                    in1=sin_v[:, :, 0, :],
-                    op0=MULT,
-                    op1=MULT,
-                )
-                for i in range(ROUND_PASSES):
-                    qr_t = flipped.tile([P, PACK, P], F32)
-                    for u in range(2):
-                        for e in range(2):
-                            h = 2 * i + u
-                            nc.tensor.matmul(
-                                out=qr_t[:, 2 * u + e, :],
-                                lhsT=direct[:, h, e, :],
-                                rhs=identity[:],
-                                is_transpose=True,
-                                start=True,
-                                stop=False,
-                            )
-                            nc.tensor.matmul(
-                                out=qr_t[:, 2 * u + e, :],
-                                lhsT=crossed[:, h, e, :],
-                                rhs=identity[:],
-                                is_transpose=True,
-                                start=False,
-                                stop=True,
-                            )
-                    nc.scalar.copy(
-                        out=qr_grouped[i][:, tt, :, :], in_=qr_t[:].rearrange("p j t -> p t j")
-                    )
+        def load(s):
+            g_in = grad_in.tile([P, PACK, VALUES], BF16)
+            nc.sync.dma_start(
+                out=g_in[:].rearrange("p (u e) d -> p u e d", u=2),
+                in_=g_dram[s * K_PASS : (s + 1) * K_PASS, :].rearrange(
+                    "(u p e) d -> p u e d", u=2, p=P, e=2
+                ),
+            )
+            grad_loaded[s] = g_in
+            if s % LOAD_STEPS < TOKEN_TILES:
+                tt = s % LOAD_STEPS
+                chunk = s // LOAD_STEPS
+                rows = slice(tt * P, (tt + 1) * P)
+                cols = slice(chunk * LOAD_FEATURES, (chunk + 1) * LOAD_FEATURES)
+                q_in = rope_in.tile([P, LOAD_FEATURES], BF16)
+                nc.sync.dma_start(out=q_in[:], in_=q_dram[rows, cols])
+                cos_in = rope_in.tile([P, LOAD_FEATURES], BF16)
+                nc.sync.dma_start(out=cos_in[:], in_=cos[rows, cols])
+                sin_in = rope_in.tile([P, LOAD_FEATURES], BF16)
+                nc.sync.dma_start(out=sin_in[:], in_=sin[rows, cols])
+                rope_loaded[(chunk, tt)] = (q_in, cos_in, sin_in)
 
-            for i in range(ROUND_PASSES):
-                g = r * ROUND_PASSES + i
-                g_bf = grouped.tile([P, VALUES, PACK], BF16, align_bytes=64)
+        def rope_products(s):
+            tt = s % TOKEN_TILES
+            first = (s // TOKEN_TILES) * STEP_FEATURES
+            chunk = first // LOAD_FEATURES
+            first = first % LOAD_FEATURES
+            q_v, cos_v, sin_v = [
+                t[:, first : first + STEP_FEATURES].rearrange(
+                    "t (h p e) -> t h e p", h=HALVES, p=P, e=2
+                )
+                for t in rope_loaded[(chunk, tt)]
+            ]
+            direct = planes.tile([P, HALVES, 2, P], F32)
+            nc.vector.tensor_tensor(out=direct[:], in0=q_v, in1=cos_v, op=MULT)
+            crossed = planes.tile([P, HALVES, 2, P], F32)
+            nc.vector.tensor_tensor(
+                out=crossed[:, :, 1, :], in0=q_v[:, :, 0, :], in1=sin_v[:, :, 1, :], op=MULT
+            )
+            nc.vector.scalar_tensor_tensor(
+                out=crossed[:, :, 0, :],
+                in0=q_v[:, :, 1, :],
+                scalar=-1.0,
+                in1=sin_v[:, :, 0, :],
+                op0=MULT,
+                op1=MULT,
+            )
+            products[s] = (direct, crossed)
+
+        def transpose_add(s):
+            direct, crossed = products[s]
+            banks[s] = []
+            for i in range(STEP_PASSES):
+                qr_t = flipped.tile([P, PACK, P], F32)
+                for j in range(PACK):
+                    h = 2 * i + j // 2
+                    e = j % 2
+                    nc.tensor.matmul(
+                        out=qr_t[:, j, :],
+                        lhsT=direct[:, h, e, :],
+                        rhs=identity[:],
+                        is_transpose=True,
+                        start=True,
+                        stop=False,
+                    )
+                    nc.tensor.matmul(
+                        out=qr_t[:, j, :],
+                        lhsT=crossed[:, h, e, :],
+                        rhs=identity[:],
+                        is_transpose=True,
+                        start=False,
+                        stop=True,
+                    )
+                banks[s].append(qr_t)
+
+        def evacuate(s):
+            qr_bf = grouped.tile([P, STEP_PASSES, P, PACK], BF16, align_bytes=64)
+            for i in range(STEP_PASSES):
                 nc.scalar.copy(
-                    out=g_bf[:].rearrange("p (c i) j -> p c j i", i=4),
-                    in_=grad_tiles[i][:].rearrange("p j (c i) -> p c j i", i=4),
+                    out=qr_bf[:, i, :, :], in_=banks[s][i][:].rearrange("p j t -> p t j")
                 )
-                g_codes = packed.tile([P, VALUES], U32, align_bytes=64)
-                g_scales = packed.tile([P, VALUES], U8, align_bytes=64)
-                nc.vector.quantize_mx(
-                    out=g_codes[:].bitcast(E5M2_X4),
-                    scales=g_scales[:],
-                    in_=g_bf[:].rearrange("p d j -> p (d j)"),
-                )
-                q_codes = packed.tile([P, TOKENS], U32, align_bytes=64)
-                q_scales = packed.tile([P, TOKENS], U8, align_bytes=64)
-                nc.vector.quantize_mx(
-                    out=q_codes[:].bitcast(E4M3_X4),
-                    scales=q_scales[:],
-                    in_=qr_grouped[i][:].rearrange("p a t j -> p (a t j)"),
-                )
-                for tt in range(TOKEN_TILES):
-                    tok = slice(tt * P, (tt + 1) * P)
-                    nc.tensor.matmul_mx(
-                        out=acc[tt][:],
-                        lhsT=q_codes[:, tok].bitcast(E4M3_X4),
-                        lhsT_scale=q_scales[:, tok],
-                        rhs=g_codes[:].bitcast(E5M2_X4),
-                        rhs_scale=g_scales[:],
-                        start=(g == 0),
-                        stop=(g == PASSES - 1),
-                    )
+            rope_bf[s] = qr_bf
 
-        out0 = result.tile([P, VALUES], F32)
-        nc.vector.tensor_scalar_mul(out=out0[:], in0=acc[0][:], scalar1=SCALE)
-        nc.sync.dma_start(out=out_dram[0:P, :], in_=out0[:])
-        out1 = result.tile([P, VALUES], F32)
-        nc.scalar.mul(out=out1[:], in_=acc[1][:], mul=SCALE)
-        nc.sync.dma_start(out=out_dram[P : 2 * P, :], in_=out1[:])
+        def regroup_grad(s):
+            g_bf = grouped.tile([P, VALUES, PACK], BF16, align_bytes=64)
+            nc.scalar.copy(
+                out=g_bf[:].rearrange("p (c i) j -> p c j i", i=4),
+                in_=grad_loaded[s][:].rearrange("p j (c i) -> p c j i", i=4),
+            )
+            grad_bf[s] = g_bf
+
+        def quantise_grad(s):
+            g_codes = grad_mx.tile([P, VALUES], U32, align_bytes=64)
+            g_scales = grad_mx.tile([P, VALUES], U8, align_bytes=64)
+            nc.vector.quantize_mx(
+                out=g_codes[:].bitcast(E5M2_X4),
+                scales=g_scales[:],
+                in_=grad_bf[s][:].rearrange("p d j -> p (d j)"),
+            )
+            grad_packed[s] = (g_codes, g_scales)
+
+        def quantise_rope(s):
+            q_codes = rope_mx.tile([P, STEP_PASSES * P], U32, align_bytes=64)
+            q_scales = rope_mx.tile([P, STEP_PASSES * P], U8, align_bytes=64)
+            nc.vector.quantize_mx(
+                out=q_codes[:].bitcast(E4M3_X4),
+                scales=q_scales[:],
+                in_=rope_bf[s][:].rearrange("p i t j -> p (i t j)"),
+            )
+            rope_packed[s] = (q_codes, q_scales)
+
+        def multiply(s):
+            tt = s % TOKEN_TILES
+            q_codes, q_scales = rope_packed[s]
+            for i in range(STEP_PASSES):
+                g = (s // TOKEN_TILES) * STEP_PASSES + i
+                g_codes, g_scales = grad_packed[g]
+                tokens = slice(i * P, (i + 1) * P)
+                nc.tensor.matmul_mx(
+                    out=acc[tt][:],
+                    lhsT=q_codes[:, tokens].bitcast(E4M3_X4),
+                    lhsT_scale=q_scales[:, tokens],
+                    rhs=g_codes[:].bitcast(E5M2_X4),
+                    rhs_scale=g_scales[:],
+                    start=(g == 0),
+                    stop=(g == PASSES - 1),
+                )
+
+        def run(stage, s):
+            if 0 <= s < STEPS:
+                stage(s)
+
+        with tc.manual_schedule():
+            for turn in range(-LOAD_AHEAD, STEPS + 5):
+                run(load, turn + LOAD_AHEAD)
+                run(multiply, turn - 4)
+                run(rope_products, turn)
+                run(transpose_add, turn)
+                run(regroup_grad, turn)
+                run(evacuate, turn - 2)
+                run(quantise_grad, turn - 1)
+                run(quantise_rope, turn - 3)
+
+            out0 = result.tile([P, VALUES], F32)
+            nc.vector.tensor_scalar_mul(out=out0[:], in0=acc[0][:], scalar1=SCALE)
+            nc.sync.dma_start(out=out_dram[0:P, :], in_=out0[:])
+            out1 = result.tile([P, VALUES], F32)
+            nc.scalar.mul(out=out1[:], in_=acc[1][:], mul=SCALE)
+            nc.sync.dma_start(out=out_dram[P : 2 * P, :], in_=out1[:])

@@ -25,9 +25,7 @@ STEP_PASSES = 2
 STEP_FEATURES = STEP_PASSES * K_PASS
 STEPS = TOKEN_TILES * PASSES // STEP_PASSES
 HALVES = 2 * STEP_PASSES
-LOAD_FEATURES = 2 * STEP_FEATURES
-LOAD_STEPS = TOKEN_TILES * LOAD_FEATURES // STEP_FEATURES
-LOAD_AHEAD = 4
+LOAD_AHEAD = 6
 
 FLOPS = 2 * TOKENS * FEATURES * VALUES
 BYTES = 2 * (3 * TOKENS * FEATURES + FEATURES * VALUES) + 4 * TOKENS * VALUES
@@ -41,7 +39,7 @@ def tile_attention_pb_kernel(tc, Q, V, state, cos, sin, grad_out, out):
 
     with ExitStack() as pools:
         const = pools.enter_context(tc.tile_pool(name="const", bufs=1))
-        rope_in = pools.enter_context(tc.tile_pool(name="rope_in", bufs=4))
+        rope_in = pools.enter_context(tc.tile_pool(name="rope_in", bufs=LOAD_AHEAD + 2))
         grad_in = pools.enter_context(tc.tile_pool(name="grad_in", bufs=LOAD_AHEAD + 2))
         planes = pools.enter_context(tc.tile_pool(name="planes", bufs=3))
         grouped = pools.enter_context(tc.tile_pool(name="grouped", bufs=3))
@@ -77,29 +75,20 @@ def tile_attention_pb_kernel(tc, Q, V, state, cos, sin, grad_out, out):
                 ),
             )
             grad_loaded[s] = g_in
-            if s % LOAD_STEPS < TOKEN_TILES:
-                tt = s % LOAD_STEPS
-                chunk = s // LOAD_STEPS
-                rows = slice(tt * P, (tt + 1) * P)
-                cols = slice(chunk * LOAD_FEATURES, (chunk + 1) * LOAD_FEATURES)
-                q_in = rope_in.tile([P, LOAD_FEATURES], BF16)
-                nc.sync.dma_start(out=q_in[:], in_=q_dram[rows, cols])
-                cos_in = rope_in.tile([P, LOAD_FEATURES], BF16)
-                nc.sync.dma_start(out=cos_in[:], in_=cos[rows, cols])
-                sin_in = rope_in.tile([P, LOAD_FEATURES], BF16)
-                nc.sync.dma_start(out=sin_in[:], in_=sin[rows, cols])
-                rope_loaded[(chunk, tt)] = (q_in, cos_in, sin_in)
+            rows = slice((s % TOKEN_TILES) * P, (s % TOKEN_TILES + 1) * P)
+            first = (s // TOKEN_TILES) * STEP_FEATURES
+            cols = slice(first, first + STEP_FEATURES)
+            q_in = rope_in.tile([P, STEP_FEATURES], BF16)
+            nc.sync.dma_start(out=q_in[:], in_=q_dram[rows, cols])
+            cos_in = rope_in.tile([P, STEP_FEATURES], BF16)
+            nc.sync.dma_start(out=cos_in[:], in_=cos[rows, cols])
+            sin_in = rope_in.tile([P, STEP_FEATURES], BF16)
+            nc.sync.dma_start(out=sin_in[:], in_=sin[rows, cols])
+            rope_loaded[s] = (q_in, cos_in, sin_in)
 
         def rope_products(s):
-            tt = s % TOKEN_TILES
-            first = (s // TOKEN_TILES) * STEP_FEATURES
-            chunk = first // LOAD_FEATURES
-            first = first % LOAD_FEATURES
             q_v, cos_v, sin_v = [
-                t[:, first : first + STEP_FEATURES].rearrange(
-                    "t (h p e) -> t h e p", h=HALVES, p=P, e=2
-                )
-                for t in rope_loaded[(chunk, tt)]
+                t[:].rearrange("t (h p e) -> t h e p", h=HALVES, p=P, e=2) for t in rope_loaded[s]
             ]
             direct = planes.tile([P, HALVES, 2, P], F32)
             nc.vector.tensor_tensor(out=direct[:], in0=q_v, in1=cos_v, op=MULT)
@@ -153,10 +142,12 @@ def tile_attention_pb_kernel(tc, Q, V, state, cos, sin, grad_out, out):
 
         def regroup_grad(s):
             g_bf = grouped.tile([P, VALUES, PACK], BF16, align_bytes=64)
-            nc.scalar.copy(
-                out=g_bf[:].rearrange("p (c i) j -> p c j i", i=4),
-                in_=grad_loaded[s][:].rearrange("p j (c i) -> p c j i", i=4),
-            )
+            dst = g_bf[:].rearrange("p (c i) j -> p c j i", i=4)
+            src = grad_loaded[s][:].rearrange("p j (c i) -> p c j i", i=4)
+            if s == STEPS - 1:
+                nc.vector.tensor_copy(out=dst, in_=src)
+            else:
+                nc.scalar.copy(out=dst, in_=src)
             grad_bf[s] = g_bf
 
         def quantise_grad(s):

@@ -41,10 +41,10 @@ def tile_attention_pb_kernel(tc, Q, V, state, cos, sin, grad_out, out):
         const = pools.enter_context(tc.tile_pool(name="const", bufs=1))
         rope_in = pools.enter_context(tc.tile_pool(name="rope_in", bufs=LOAD_AHEAD + 2))
         grad_in = pools.enter_context(tc.tile_pool(name="grad_in", bufs=LOAD_AHEAD + 2))
-        planes = pools.enter_context(tc.tile_pool(name="planes", bufs=3))
-        grouped = pools.enter_context(tc.tile_pool(name="grouped", bufs=3))
-        grad_mx = pools.enter_context(tc.tile_pool(name="grad_mx", bufs=6))
-        rope_mx = pools.enter_context(tc.tile_pool(name="rope_mx", bufs=3))
+        planes = pools.enter_context(tc.tile_pool(name="planes", bufs=4))
+        grouped = pools.enter_context(tc.tile_pool(name="grouped", bufs=4))
+        grad_mx = pools.enter_context(tc.tile_pool(name="grad_mx", bufs=PASSES))
+        rope_mx = pools.enter_context(tc.tile_pool(name="rope_mx", bufs=STEPS))
         result = pools.enter_context(tc.tile_pool(name="result", bufs=1))
         flipped = pools.enter_context(tc.psum_pool(name="flipped", bufs=6))
         sums = pools.enter_context(tc.psum_pool(name="sums", bufs=1))

@@ -21,11 +21,11 @@ TOKEN_TILES = TOKENS // P
 PASSES = FEATURES // K_PASS
 SCALE = FEATURES**-0.5
 
-STEP_PASSES = 2
-STEP_FEATURES = STEP_PASSES * K_PASS
-STEPS = TOKEN_TILES * PASSES // STEP_PASSES
-HALVES = 2 * STEP_PASSES
+GROUP_PASSES = (1, 1, 2, 2, 2, 2, 2, 2, 2)
+assert sum(GROUP_PASSES) == PASSES and max(GROUP_PASSES) <= TOKEN_TILES
+STEPS = TOKEN_TILES * len(GROUP_PASSES)
 LOAD_AHEAD = 6
+VECTOR_PASSES = (PASSES - 1,)
 
 FLOPS = 2 * TOKENS * FEATURES * VALUES
 BYTES = 2 * (3 * TOKENS * FEATURES + FEATURES * VALUES) + 4 * TOKENS * VALUES
@@ -36,6 +36,12 @@ def tile_attention_pb_kernel(tc, Q, V, state, cos, sin, grad_out, out):
     q_dram = Q.flatten_outer_dims()
     g_dram = grad_out.flatten_outer_dims()
     out_dram = out.flatten_outer_dims()
+
+    steps = []
+    for group, count in enumerate(GROUP_PASSES):
+        first_pass = sum(GROUP_PASSES[:group])
+        for tt in range(TOKEN_TILES):
+            steps.append((tt, first_pass, count, first_pass + tt if tt < count else None))
 
     with ExitStack() as pools:
         const = pools.enter_context(tc.tile_pool(name="const", bufs=1))
@@ -65,34 +71,40 @@ def tile_attention_pb_kernel(tc, Q, V, state, cos, sin, grad_out, out):
         grad_bf = {}
         rope_packed = {}
         grad_packed = {}
+        multiplied = []
 
-        def load(s):
+        def load_grad(g):
             g_in = grad_in.tile([P, PACK, VALUES], BF16)
             nc.sync.dma_start(
                 out=g_in[:].rearrange("p (u e) d -> p u e d", u=2),
-                in_=g_dram[s * K_PASS : (s + 1) * K_PASS, :].rearrange(
+                in_=g_dram[g * K_PASS : (g + 1) * K_PASS, :].rearrange(
                     "(u p e) d -> p u e d", u=2, p=P, e=2
                 ),
             )
-            grad_loaded[s] = g_in
-            rows = slice((s % TOKEN_TILES) * P, (s % TOKEN_TILES + 1) * P)
-            first = (s // TOKEN_TILES) * STEP_FEATURES
-            cols = slice(first, first + STEP_FEATURES)
-            q_in = rope_in.tile([P, STEP_FEATURES], BF16)
+            grad_loaded[g] = g_in
+
+        def load(s):
+            tt, first_pass, count, g = steps[s]
+            rows = slice(tt * P, (tt + 1) * P)
+            cols = slice(first_pass * K_PASS, (first_pass + count) * K_PASS)
+            q_in = rope_in.tile([P, count * K_PASS], BF16)
             nc.sync.dma_start(out=q_in[:], in_=q_dram[rows, cols])
-            cos_in = rope_in.tile([P, STEP_FEATURES], BF16)
+            cos_in = rope_in.tile([P, count * K_PASS], BF16)
             nc.sync.dma_start(out=cos_in[:], in_=cos[rows, cols])
-            sin_in = rope_in.tile([P, STEP_FEATURES], BF16)
+            if g is not None:
+                load_grad(g)
+            sin_in = rope_in.tile([P, count * K_PASS], BF16)
             nc.sync.dma_start(out=sin_in[:], in_=sin[rows, cols])
             rope_loaded[s] = (q_in, cos_in, sin_in)
 
         def rope_products(s):
+            halves = 2 * steps[s][2]
             q_v, cos_v, sin_v = [
-                t[:].rearrange("t (h p e) -> t h e p", h=HALVES, p=P, e=2) for t in rope_loaded[s]
+                t[:].rearrange("t (h p e) -> t h e p", h=halves, p=P, e=2) for t in rope_loaded[s]
             ]
-            direct = planes.tile([P, HALVES, 2, P], F32)
+            direct = planes.tile([P, halves, 2, P], F32)
             nc.vector.tensor_tensor(out=direct[:], in0=q_v, in1=cos_v, op=MULT)
-            crossed = planes.tile([P, HALVES, 2, P], F32)
+            crossed = planes.tile([P, halves, 2, P], F32)
             nc.vector.tensor_tensor(
                 out=crossed[:, :, 1, :], in0=q_v[:, :, 0, :], in1=sin_v[:, :, 1, :], op=MULT
             )
@@ -109,7 +121,7 @@ def tile_attention_pb_kernel(tc, Q, V, state, cos, sin, grad_out, out):
         def transpose_add(s):
             direct, crossed = products[s]
             banks[s] = []
-            for i in range(STEP_PASSES):
+            for i in range(steps[s][2]):
                 qr_t = flipped.tile([P, PACK, P], F32)
                 for j in range(PACK):
                     h = 2 * i + j // 2
@@ -133,36 +145,44 @@ def tile_attention_pb_kernel(tc, Q, V, state, cos, sin, grad_out, out):
                 banks[s].append(qr_t)
 
         def evacuate(s):
-            qr_bf = grouped.tile([P, STEP_PASSES, P, PACK], BF16, align_bytes=64)
-            for i in range(STEP_PASSES):
+            count = steps[s][2]
+            qr_bf = grouped.tile([P, count, P, PACK], BF16, align_bytes=64)
+            for i in range(count):
                 nc.scalar.copy(
                     out=qr_bf[:, i, :, :], in_=banks[s][i][:].rearrange("p j t -> p t j")
                 )
             rope_bf[s] = qr_bf
 
         def regroup_grad(s):
+            g = steps[s][3]
+            if g is None:
+                return
             g_bf = grouped.tile([P, VALUES, PACK], BF16, align_bytes=64)
             dst = g_bf[:].rearrange("p (c i) j -> p c j i", i=4)
-            src = grad_loaded[s][:].rearrange("p j (c i) -> p c j i", i=4)
-            if s == STEPS - 1:
+            src = grad_loaded[g][:].rearrange("p j (c i) -> p c j i", i=4)
+            if g in VECTOR_PASSES:
                 nc.vector.tensor_copy(out=dst, in_=src)
             else:
                 nc.scalar.copy(out=dst, in_=src)
-            grad_bf[s] = g_bf
+            grad_bf[g] = g_bf
 
         def quantise_grad(s):
+            g = steps[s][3]
+            if g is None:
+                return
             g_codes = grad_mx.tile([P, VALUES], U32, align_bytes=64)
             g_scales = grad_mx.tile([P, VALUES], U8, align_bytes=64)
             nc.vector.quantize_mx(
                 out=g_codes[:].bitcast(E5M2_X4),
                 scales=g_scales[:],
-                in_=grad_bf[s][:].rearrange("p d j -> p (d j)"),
+                in_=grad_bf[g][:].rearrange("p d j -> p (d j)"),
             )
-            grad_packed[s] = (g_codes, g_scales)
+            grad_packed[g] = (g_codes, g_scales)
 
         def quantise_rope(s):
-            q_codes = rope_mx.tile([P, STEP_PASSES * P], U32, align_bytes=64)
-            q_scales = rope_mx.tile([P, STEP_PASSES * P], U8, align_bytes=64)
+            count = steps[s][2]
+            q_codes = rope_mx.tile([P, count * P], U32, align_bytes=64)
+            q_scales = rope_mx.tile([P, count * P], U8, align_bytes=64)
             nc.vector.quantize_mx(
                 out=q_codes[:].bitcast(E4M3_X4),
                 scales=q_scales[:],
@@ -171,10 +191,10 @@ def tile_attention_pb_kernel(tc, Q, V, state, cos, sin, grad_out, out):
             rope_packed[s] = (q_codes, q_scales)
 
         def multiply(s):
-            tt = s % TOKEN_TILES
+            tt, first_pass, count, unused = steps[s]
             q_codes, q_scales = rope_packed[s]
-            for i in range(STEP_PASSES):
-                g = (s // TOKEN_TILES) * STEP_PASSES + i
+            for i in range(count):
+                g = first_pass + i
                 g_codes, g_scales = grad_packed[g]
                 tokens = slice(i * P, (i + 1) * P)
                 nc.tensor.matmul_mx(
@@ -186,21 +206,30 @@ def tile_attention_pb_kernel(tc, Q, V, state, cos, sin, grad_out, out):
                     start=(g == 0),
                     stop=(g == PASSES - 1),
                 )
+            multiplied.append(s)
+
+        def multiply_what_is_ready():
+            while len(multiplied) < STEPS:
+                s = len(multiplied)
+                last_pass = steps[s][1] + steps[s][2] - 1
+                if s not in rope_packed or last_pass not in grad_packed:
+                    return
+                multiply(s)
 
         def run(stage, s):
             if 0 <= s < STEPS:
                 stage(s)
 
         with tc.manual_schedule():
-            for turn in range(-LOAD_AHEAD, STEPS + 5):
+            for turn in range(-LOAD_AHEAD, STEPS + 3):
                 run(load, turn + LOAD_AHEAD)
-                run(multiply, turn - 4)
                 run(rope_products, turn)
-                run(transpose_add, turn)
                 run(regroup_grad, turn)
-                run(evacuate, turn - 2)
+                run(transpose_add, turn)
+                run(evacuate, turn - 1)
                 run(quantise_grad, turn - 1)
-                run(quantise_rope, turn - 3)
+                run(quantise_rope, turn - 2)
+                multiply_what_is_ready()
 
             out0 = result.tile([P, VALUES], F32)
             nc.vector.tensor_scalar_mul(out=out0[:], in0=acc[0][:], scalar1=SCALE)

from contextlib import ExitStack

import concourse.mybir as mybir
from concourse.masks import make_identity

BF16 = mybir.dt.bfloat16
F32 = mybir.dt.float32
U32 = mybir.dt.uint32
U8 = mybir.dt.uint8
E4M3_X4 = mybir.dt.float8_e4m3fn_x4
E5M2_X4 = mybir.dt.float8_e5m2_x4
MULT = mybir.AluOpType.mult

P = 128
PACK = 4
K_PASS = P * PACK
TOKENS = 256
FEATURES = 8192
VALUES = 512
TOKEN_TILES = TOKENS // P
PASSES = FEATURES // K_PASS
SCALE = FEATURES**-0.5

GROUP_PASSES = (1, 1, 2, 2, 2, 2, 2, 2, 2)
assert sum(GROUP_PASSES) == PASSES and max(GROUP_PASSES) <= TOKEN_TILES
STEPS = TOKEN_TILES * len(GROUP_PASSES)
LOAD_AHEAD = 6
VECTOR_PASSES = (PASSES - 1,)

FLOPS = 2 * TOKENS * FEATURES * VALUES
BYTES = 2 * (3 * TOKENS * FEATURES + FEATURES * VALUES) + 4 * TOKENS * VALUES


def tile_attention_pb_kernel(tc, Q, V, state, cos, sin, grad_out, out):
    nc = tc.nc
    q_dram = Q.flatten_outer_dims()
    g_dram = grad_out.flatten_outer_dims()
    out_dram = out.flatten_outer_dims()

    steps = []
    for group, count in enumerate(GROUP_PASSES):
        first_pass = sum(GROUP_PASSES[:group])
        for tt in range(TOKEN_TILES):
            steps.append((tt, first_pass, count, first_pass + tt if tt < count else None))

    with ExitStack() as pools:
        const = pools.enter_context(tc.tile_pool(name="const", bufs=1))
        rope_in = pools.enter_context(tc.tile_pool(name="rope_in", bufs=LOAD_AHEAD + 2))
        grad_in = pools.enter_context(tc.tile_pool(name="grad_in", bufs=LOAD_AHEAD + 2))
        planes = pools.enter_context(tc.tile_pool(name="planes", bufs=4))
        grouped = pools.enter_context(tc.tile_pool(name="grouped", bufs=4))
        grad_mx = pools.enter_context(tc.tile_pool(name="grad_mx", bufs=PASSES))
        rope_mx = pools.enter_context(tc.tile_pool(name="rope_mx", bufs=STEPS))
        result = pools.enter_context(tc.tile_pool(name="result", bufs=1))
        flipped = pools.enter_context(tc.psum_pool(name="flipped", bufs=6))
        sums = pools.enter_context(tc.psum_pool(name="sums", bufs=1))

        identity = const.tile([P, P], F32)
        make_identity(nc, identity[:])

        acc = []
        for tt in range(TOKEN_TILES):
            acc_tile = sums.tile([P, VALUES], F32, name="acc%d" % tt)
            acc.append(acc_tile)

        rope_loaded = {}
        grad_loaded = {}
        products = {}
        banks = {}
        rope_bf = {}
        grad_bf = {}
        rope_packed = {}
        grad_packed = {}
        multiplied = []

        def load_grad(g):
            g_in = grad_in.tile([P, PACK, VALUES], BF16)
            nc.sync.dma_start(
                out=g_in[:].rearrange("p (u e) d -> p u e d", u=2),
                in_=g_dram[g * K_PASS : (g + 1) * K_PASS, :].rearrange(
                    "(u p e) d -> p u e d", u=2, p=P, e=2
                ),
            )
            grad_loaded[g] = g_in

        def load(s):
            tt, first_pass, count, g = steps[s]
            rows = slice(tt * P, (tt + 1) * P)
            cols = slice(first_pass * K_PASS, (first_pass + count) * K_PASS)
            q_in = rope_in.tile([P, count * K_PASS], BF16)
            nc.sync.dma_start(out=q_in[:], in_=q_dram[rows, cols])
            cos_in = rope_in.tile([P, count * K_PASS], BF16)
            nc.sync.dma_start(out=cos_in[:], in_=cos[rows, cols])
            if g is not None:
                load_grad(g)
            sin_in = rope_in.tile([P, count * K_PASS], BF16)
            nc.sync.dma_start(out=sin_in[:], in_=sin[rows, cols])
            rope_loaded[s] = (q_in, cos_in, sin_in)

        def rope_products(s):
            halves = 2 * steps[s][2]
            q_v, cos_v, sin_v = [
                t[:].rearrange("t (h p e) -> t h e p", h=halves, p=P, e=2) for t in rope_loaded[s]
            ]
            direct = planes.tile([P, halves, 2, P], F32)
            nc.vector.tensor_tensor(out=direct[:], in0=q_v, in1=cos_v, op=MULT)
            crossed = planes.tile([P, halves, 2, P], F32)
            nc.vector.tensor_tensor(
                out=crossed[:, :, 1, :], in0=q_v[:, :, 0, :], in1=sin_v[:, :, 1, :], op=MULT
            )
            nc.vector.scalar_tensor_tensor(
                out=crossed[:, :, 0, :],
                in0=q_v[:, :, 1, :],
                scalar=-1.0,
                in1=sin_v[:, :, 0, :],
                op0=MULT,
                op1=MULT,
            )
            products[s] = (direct, crossed)

        def transpose_add(s):
            direct, crossed = products[s]
            banks[s] = []
            for i in range(steps[s][2]):
                qr_t = flipped.tile([P, PACK, P], F32)
                for j in range(PACK):
                    h = 2 * i + j // 2
                    e = j % 2
                    nc.tensor.matmul(
                        out=qr_t[:, j, :],
                        lhsT=direct[:, h, e, :],
                        rhs=identity[:],
                        is_transpose=True,
                        start=True,
                        stop=False,
                    )
                    nc.tensor.matmul(
                        out=qr_t[:, j, :],
                        lhsT=crossed[:, h, e, :],
                        rhs=identity[:],
                        is_transpose=True,
                        start=False,
                        stop=True,
                    )
                banks[s].append(qr_t)

        def evacuate(s):
            count = steps[s][2]
            qr_bf = grouped.tile([P, count, P, PACK], BF16, align_bytes=64)
            for i in range(count):
                nc.scalar.copy(
                    out=qr_bf[:, i, :, :], in_=banks[s][i][:].rearrange("p j t -> p t j")
                )
            rope_bf[s] = qr_bf

        def regroup_grad(s):
            g = steps[s][3]
            if g is None:
                return
            g_bf = grouped.tile([P, VALUES, PACK], BF16, align_bytes=64)
            dst = g_bf[:].rearrange("p (c i) j -> p c j i", i=4)
            src = grad_loaded[g][:].rearrange("p j (c i) -> p c j i", i=4)
            if g in VECTOR_PASSES:
                nc.vector.tensor_copy(out=dst, in_=src)
            else:
                nc.scalar.copy(out=dst, in_=src)
            grad_bf[g] = g_bf

        def quantise_grad(s):
            g = steps[s][3]
            if g is None:
                return
            g_codes = grad_mx.tile([P, VALUES], U32, align_bytes=64)
            g_scales = grad_mx.tile([P, VALUES], U8, align_bytes=64)
            nc.vector.quantize_mx(
                out=g_codes[:].bitcast(E5M2_X4),
                scales=g_scales[:],
                in_=grad_bf[g][:].rearrange("p d j -> p (d j)"),
            )
            grad_packed[g] = (g_codes, g_scales)

        def quantise_rope(s):
            count = steps[s][2]
            q_codes = rope_mx.tile([P, count * P], U32, align_bytes=64)
            q_scales = rope_mx.tile([P, count * P], U8, align_bytes=64)
            nc.vector.quantize_mx(
                out=q_codes[:].bitcast(E4M3_X4),
                scales=q_scales[:],
                in_=rope_bf[s][:].rearrange("p i t j -> p (i t j)"),
            )
            rope_packed[s] = (q_codes, q_scales)

        def multiply(s):
            tt, first_pass, count, unused = steps[s]
            q_codes, q_scales = rope_packed[s]
            for i in range(count):
                g = first_pass + i
                g_codes, g_scales = grad_packed[g]
                tokens = slice(i * P, (i + 1) * P)
                nc.tensor.matmul_mx(
                    out=acc[tt][:],
                    lhsT=q_codes[:, tokens].bitcast(E4M3_X4),
                    lhsT_scale=q_scales[:, tokens],
                    rhs=g_codes[:].bitcast(E5M2_X4),
                    rhs_scale=g_scales[:],
                    start=(g == 0),
                    stop=(g == PASSES - 1),
                )
            multiplied.append(s)

        def multiply_what_is_ready():
            while len(multiplied) < STEPS:
                s = len(multiplied)
                last_pass = steps[s][1] + steps[s][2] - 1
                if s not in rope_packed or last_pass not in grad_packed:
                    return
                multiply(s)

        def run(stage, s):
            if 0 <= s < STEPS:
                stage(s)

        with tc.manual_schedule():
            for turn in range(-LOAD_AHEAD, STEPS + 3):
                run(load, turn + LOAD_AHEAD)
                run(rope_products, turn)
                run(regroup_grad, turn)
                run(transpose_add, turn)
                run(evacuate, turn - 1)
                run(quantise_grad, turn - 1)
                run(quantise_rope, turn - 2)
                multiply_what_is_ready()

            out0 = result.tile([P, VALUES], F32)
            nc.vector.tensor_scalar_mul(out=out0[:], in0=acc[0][:], scalar1=SCALE)
            nc.sync.dma_start(out=out_dram[0:P, :], in_=out0[:])
            out1 = result.tile([P, VALUES], F32)
            nc.scalar.mul(out=out1[:], in_=acc[1][:], mul=SCALE)
            nc.sync.dma_start(out=out_dram[P : 2 * P, :], in_=out1[:])
